import numpy as np
import ml_dtypes


def mxq(x, axis, fmt="e4m3"):
    dtype, down = {"e4m3": (ml_dtypes.float8_e4m3fn, 7), "e5m2": (ml_dtypes.float8_e5m2, 14)}[fmt]
    v = np.moveaxis(np.asarray(x, np.float32).astype(ml_dtypes.bfloat16).astype(np.float64), axis, -1)
    blocks = v.reshape(v.shape[:-1] + (-1, 32))
    amax = np.abs(blocks).max(-1, keepdims=True)
    byte = np.maximum(np.where(amax > 0, np.frexp(amax)[1] - 1 + 127, 0) - down, 1)
    scale = np.exp2(byte - 127.0)
    codes = (blocks / scale).astype(np.float32).astype(dtype).astype(np.float64)
    return np.moveaxis((codes * scale).reshape(v.shape), -1, axis)


WIDE = False


def mx_kscale(k):
    if not WIDE:
        return np.ones(k)
    levels = np.array([10, -10, 5, -5, 0])
    if k % 512:
        return np.exp2(np.random.permutation(np.resize(levels, k // 32))).repeat(32)
    a = np.empty((k // 512, 16))
    for p in range(k // 512):
        a[p, :8] = np.random.permutation(np.resize(levels, 8))
        for g in range(8):
            far = levels[np.abs(levels - a[p, g]) >= 10]
            a[p, g + 8] = far[np.random.randint(len(far))]
    return np.exp2(a.ravel()).repeat(32)


BF16 = ml_dtypes.bfloat16


def bf(x):
    return np.asarray(x, np.float32).astype(BF16)


def f64(x):
    return np.asarray(x).astype(np.float64)


B, S, H, DH, C = 2, 1024, 2048, 256, 512
SCALE_BASE = 2.0 ** 9


def rotate_every_two(y):
    y1 = y[..., ::2]
    y2 = y[..., 1::2]
    return np.stack((-y2, y1), axis=-1).reshape(y.shape)


def xpos(y, downscale):
    L, D = y.shape[-2], y.shape[-1]
    d = D // 2
    scale_vec = (np.arange(0, D, 2) + 0.4 * D) / (1.4 * D)
    min_pos = (-L) // 2
    power = np.arange(min_pos, L + min_pos) / SCALE_BASE
    scale = scale_vec ** power[:, None]
    inv_freq = 1.0 / (10000.0 ** (np.arange(d) / d))
    sinusoid = np.arange(L)[:, None] * inv_freq
    sin, cos = np.sin(sinusoid), np.cos(sinusoid)
    if downscale:
        scale = 1.0 / scale
    sin = np.repeat(sin * scale, 2, axis=-1)
    cos = np.repeat(cos * scale, 2, axis=-1)
    return y * cos + rotate_every_two(y) * sin


def draw0():
    s = mx_kscale(H)
    return {"x": bf(np.random.standard_normal((B, S, H)) * s),
            "w_q": bf(np.random.standard_normal((H, DH)) * 0.5 / np.sqrt(H) / s[:, None]),
            "w_k": bf(np.random.standard_normal((H, DH)) * 0.5 / np.sqrt(H) / s[:, None]),
            "w_v": bf(np.random.standard_normal((H, DH)) * 0.25 / np.sqrt(H) / s[:, None])}


def core(x, w_q, w_k, w_v):
    xq = mxq(f64(x), 2, "e4m3")
    q = xpos(xq @ mxq(f64(w_q), 0, "e4m3"), False)
    k = xpos(xq @ mxq(f64(w_k), 0, "e4m3"), True)
    v = xq @ mxq(f64(w_v), 0, "e4m3")
    return q, k, v


def e4m3fn_bytes(y):
    return np.clip(np.asarray(y, np.float64), -448.0, 448.0).astype(np.float32).astype(ml_dtypes.float8_e4m3fn).view(np.uint8)


def e4m3fn_values(b):
    return np.asarray(b, np.uint8).view(ml_dtypes.float8_e4m3fn).astype(np.float64)


def setup_inputs():
    d = draw0()
    x0 = np.asarray(d['x']).astype(np.float64)
    s = (np.max(np.abs(x0), axis=(0, 1), keepdims=True) / 448.0).astype(np.float32)
    out = {}
    for k, v in d.items():
        if k == 'x':
            out['x_bytes'] = e4m3fn_bytes(x0 / s.astype(np.float64))
            out['x_scale'] = s
        else:
            out[k] = v
    return out


def reference(x_bytes, x_scale, w_q, w_k, w_v):
    return core(e4m3fn_values(x_bytes) * x_scale.astype(np.float64), w_q, w_k, w_v)

@@ -1,0 +1,335 @@
+from contextlib import ExitStack
+import math
+
+import concourse.mybir as mybir
+from concourse.masks import make_identity
+
+F32 = mybir.dt.float32
+BF16 = mybir.dt.bfloat16
+U8 = mybir.dt.uint8
+U32 = mybir.dt.uint32
+I32 = mybir.dt.int32
+FP8 = mybir.dt.float8_e4m3fn
+FP8X4 = mybir.dt.float8_e4m3fn_x4
+ALU = mybir.AluOpType
+ACT = mybir.ActivationFunctionType
+
+B, S, H, DH = 2, 1024, 2048, 256
+P = 128
+NT = S // P
+NG = H // 512
+NJ = DH // 2
+FLOPS = 2 * B * S * H * 3 * DH
+
+TWO_PI_HI = 6.28125
+TWO_PI_LO = 2.0 * math.pi - TWO_PI_HI
+FREQ_RATIO = 10000.0 ** (-1.0 / NJ)
+HEAVY = (0, 1, 2, 6, 7)
+
+
+def tile_retblock_pa_kernel(tc, x_bytes, x_scale, w_q, w_k, w_v, out_0, out_1, out_2):
+    nc = tc.nc
+    with ExitStack() as ctx:
+        const = ctx.enter_context(tc.tile_pool(name="const", bufs=1))
+        work = ctx.enter_context(tc.tile_pool(name="work", bufs=2))
+        psx = ctx.enter_context(tc.psum_pool(name="psx", bufs=4))
+        psa = ctx.enter_context(tc.psum_pool(name="psa", bufs=3))
+        psv = ctx.enter_context(tc.psum_pool(name="psv", bufs=1))
+        ctx.enter_context(tc.manual_schedule())
+
+        xv = x_bytes.rearrange("b (s p) k -> s p b k", p=P)
+        xb8 = []
+        for s in range(NT):
+            xbytes = const.tile([P, B, H], U8, name="xbytes%d" % s)
+            xb8.append(xbytes)
+        wraw = []
+        for m in range(3):
+            wr = const.tile([P, NG, 4, DH], BF16, name="wraw%d" % m)
+            wraw.append(wr)
+        for g in range(NG):
+            nc.sync.dma_start(out=xb8[0][:, :, 512 * g:512 * (g + 1)], in_=xv[0][:, :, 512 * g:512 * (g + 1)])
+        scl = const.tile([P, NG * 4], F32, name="scl")
+        nc.sync.dma_start(
+            out=scl[:].rearrange("p (g t) -> p g t", t=4),
+            in_=x_scale.rearrange("a b k -> (a b k)").rearrange("(g p t) -> p g t", p=P, t=4),
+        )
+        nc.sync.dma_start(out=xb8[1][:], in_=xv[1])
+        for g in range(NG):
+            for m, w in enumerate((w_q, w_k, w_v)):
+                nc.sync.dma_start(
+                    out=wraw[m][:, g], in_=w.rearrange("(g p t) n -> p g t n", p=P, t=4)[:, g]
+                )
+        for s in range(2, NT):
+            nc.sync.dma_start(out=xb8[s][:], in_=xv[s])
+
+        ident = const.tile([P, P], F32, name="ident")
+        make_identity(nc, ident[:])
+        pos = const.tile([P, NT], F32, name="pos")
+        nc.gpsimd.iota(pos[:], pattern=[[P, NT]], base=0, channel_multiplier=1,
+                       allow_small_or_imprecise_dtypes=True)
+        jj = const.tile([P, NJ], F32, name="jj")
+        nc.gpsimd.iota(jj[:], pattern=[[1, NJ]], base=0, channel_multiplier=0,
+                       allow_small_or_imprecise_dtypes=True)
+
+        th = const.tile([P, NJ], F32, name="th")
+        nc.vector.memset(th[:, 0:1], 1.0)
+        m = 1
+        while m < NJ:
+            nc.vector.tensor_scalar(out=th[:, m:2 * m], in0=th[:, 0:m], scalar1=FREQ_RATIO ** m,
+                                    scalar2=None, op0=ALU.mult)
+            m *= 2
+        cj = const.tile([P, NJ], F32, name="cj")
+        nc.vector.tensor_scalar(out=cj[:], in0=jj[:], scalar1=2.0 / (1.4 * DH),
+                                scalar2=(0.4 * DH) / (1.4 * DH), op0=ALU.mult, op1=ALU.add)
+        pc = const.tile([P, NT], F32, name="pc")
+        nc.vector.tensor_scalar(out=pc[:], in0=pos[:], scalar1=-0.5 * S, scalar2=1.0 / 512.0,
+                                op0=ALU.add, op1=ALU.mult)
+        hpi = const.tile([P, 1], F32, name="hpi")
+        nc.vector.tensor_scalar(out=hpi[:], in0=th[:, 0:1], scalar1=0.5 * math.pi, scalar2=None,
+                                op0=ALU.mult)
+        lnc = const.tile([P, NJ], F32, name="lnc")
+        nc.scalar.activation(out=lnc[:], in_=cj[:], func=ACT.Ln)
+
+        TSH = [P, NT, NJ]
+        ang = const.tile(TSH, F32, name="ang", tag="ta")
+        nc.vector.tensor_tensor(out=ang[:], in0=th[:].unsqueeze(1).to_broadcast(TSH),
+                                in1=pos[:].unsqueeze(2).to_broadcast(TSH), op=ALU.mult)
+        ki = const.tile(TSH, I32, name="ki", tag="tb")
+        r1 = const.tile(TSH, F32, name="r1", tag="tc")
+        red = const.tile(TSH, F32, name="red", tag="td")
+
+        def reduce_angles(step):
+            if step == 0:
+                nc.vector.tensor_scalar(out=ki[:], in0=ang[:], scalar1=1.0 / (2.0 * math.pi), scalar2=None,
+                                        op0=ALU.mult)
+            if step == 1:
+                nc.vector.scalar_tensor_tensor(out=r1[:], in0=ki[:], scalar=-TWO_PI_HI, in1=ang[:],
+                                               op0=ALU.mult, op1=ALU.add)
+            if step == 2:
+                nc.vector.scalar_tensor_tensor(out=red[:], in0=ki[:], scalar=-TWO_PI_LO, in1=r1[:],
+                                               op0=ALU.mult, op1=ALU.add)
+
+        zz = const.tile([P, NT, 2, NJ], F32, name="zz")
+        cz = const.tile([P, NT, 2, NJ], F32, name="cz")
+        sz = const.tile([P, NT, 2, NJ], F32, name="sz")
+
+        wgqk = const.tile([P, NG, 2048], BF16, name="wgqk", align_bytes=64)
+        wgv = const.tile([P, NG, 1024], BF16, name="wgv", align_bytes=64)
+        wcqk = const.tile([P, NG, 512], U32, name="wcqk", align_bytes=64)
+        wsqk = const.tile([P, NG, 512], U8, name="wsqk", align_bytes=64)
+        wcv = const.tile([P, NG, 256], U32, name="wcv", align_bytes=64)
+        wsv = const.tile([P, NG, 256], U8, name="wsv", align_bytes=64)
+
+        xbfs, xts, grps, xcs, xss, accs, accvs, ysws, ress = {}, {}, {}, {}, {}, {}, {}, {}, {}
+
+        def cast(s, chunks):
+            xbf = work.tile([P, B, H], BF16, name="xbf", tag="xbf", bufs=3)
+            xbfs[s] = xbf
+            w = H // chunks
+            if chunks == 1:
+                nc.scalar.activation(out=xbf[:].rearrange("p b k -> p (b k)"),
+                               in_=xb8[s][:].rearrange("p b k -> p (b k)").bitcast(FP8), func=ACT.Copy)
+            else:
+                for c in range(chunks):
+                    for b in range(B):
+                        nc.scalar.activation(out=xbf[:, b, c * w:(c + 1) * w],
+                                       in_=xb8[s][:, b, c * w:(c + 1) * w].bitcast(FP8), func=ACT.Copy)
+
+        def transposes(s, g):
+            xt = psx.tile([P, 2, B * P], F32, name="xt", tag="xt")
+            xts[(s, g)] = xt
+            for b in range(B):
+                words = xbfs[s][:, b, :].bitcast(F32)
+                for u in range(2):
+                    nc.tensor.transpose(xt[:, u, P * b:P * (b + 1)],
+                                        words[:, 256 * g + u:256 * (g + 1):2], ident[:])
+
+        def evacuate(s, g):
+            if g == 0:
+                grp = work.tile([P, NG, 1024], BF16, name="grp", tag="grp", bufs=2, align_bytes=64)
+                grps[s] = grp
+            nc.vector.tensor_tensor(
+                out=grps[s][:, g, :].rearrange("p (r u e) -> p r u e", u=2, e=2),
+                in0=xts[(s, g)][:].rearrange("p u r -> p (u r)").bitcast(BF16).rearrange(
+                    "p (u r e) -> p r u e", u=2, e=2),
+                in1=scl[:, 4 * g:4 * g + 4].rearrange("p (u e) -> p u e", u=2).unsqueeze(1)
+                .to_broadcast([P, B * P, 2, 2]),
+                op=ALU.mult,
+            )
+
+        def quantize(s, h):
+            if h == 0:
+                xc = work.tile([P, NG, B * P], U32, name="xc", tag="xc", bufs=4, align_bytes=64)
+                xs = work.tile([P, NG, B * P], U8, name="xs", tag="xs", bufs=4, align_bytes=64)
+                xcs[s], xss[s] = xc, xs
+            gs = slice(2 * h, 2 * h + 2)
+            nc.vector.quantize_mx(
+                out=xcs[s][:, gs, :].rearrange("p g c -> p (g c)").bitcast(FP8X4),
+                scales=xss[s][:, gs, :].rearrange("p g c -> p (g c)"),
+                in_=grps[s][:, gs, :].rearrange("p g c -> p (g c)"),
+            )
+
+        def multiply(s, k):
+            xc, xs = xcs[s], xss[s]
+            b, h = k // 2, k % 2
+            if k == 0:
+                accv = psv.tile([P, B, DH], F32, name="accv", tag="accv")
+                accvs[s] = accv
+            if h == 0:
+                acc = psa.tile([P, 2 * DH], F32, name="acc", tag="acc")
+                accs[(s, b)] = acc
+            cols = slice(P * b, P * (b + 1))
+            for g in (2 * h, 2 * h + 1):
+                nc.tensor.matmul_mx(out=accs[(s, b)][:], lhsT=xc[:, g, cols].bitcast(FP8X4),
+                                    lhsT_scale=xs[:, g, cols],
+                                    rhs=wcqk[:, g, :].bitcast(FP8X4), rhs_scale=wsqk[:, g, :],
+                                    start=(g == 0), stop=(g == NG - 1))
+                nc.tensor.matmul_mx(out=accvs[s][:, b, :], lhsT=xc[:, g, cols].bitcast(FP8X4),
+                                    lhsT_scale=xs[:, g, cols],
+                                    rhs=wcv[:, g, :].bitcast(FP8X4), rhs_scale=wsv[:, g, :],
+                                    start=(g == 0), stop=(g == NG - 1))
+
+        def table_products(h):
+            ts = slice(2 * h, 2 * h + 2)
+            nc.gpsimd.tensor_tensor(out=cz[:, ts], in0=cs[:, ts].unsqueeze(2).to_broadcast([P, 2, 2, NJ]),
+                                    in1=zz[:, ts], op=ALU.mult)
+            nc.gpsimd.tensor_tensor(out=sz[:, ts], in0=sn[:, ts].unsqueeze(2).to_broadcast([P, 2, 2, NJ]),
+                                    in1=zz[:, ts], op=ALU.mult)
+
+        oq = out_0.rearrange("b (s p) c -> s p b c", p=P)
+        ok = out_1.rearrange("b (s p) c -> s p b c", p=P)
+        ov = out_2.rearrange("b (s p) c -> s p b c", p=P)
+
+        def swapped_copy(s, b):
+            if s in HEAVY:
+                return
+            y = accs[(s, b)][:].rearrange("p (q e j) -> p q e j", q=2, e=2)
+            ysw = work.tile([P, 2, 2, NJ], F32, name="ysw", tag="ysw", bufs=4)
+            ysws[(s, b)] = ysw
+            nc.scalar.activation(out=ysw[:, :, 0, :], in_=y[:, :, 1, :], func=ACT.Copy, scale=-1.0)
+            nc.scalar.copy(out=ysw[:, :, 1, :], in_=y[:, :, 0, :])
+
+        def v_out(s):
+            resv = work.tile([P, B, DH], F32, name="resv", tag="resv", bufs=2)
+            nc.scalar.copy(out=resv[:], in_=accvs[s][:])
+            nc.sync.dma_start(out=ov[s], in_=resv[:])
+
+        def rotate(s, b):
+            if b == 0:
+                res = work.tile([P, B, 2, DH], F32, name="res", tag="res", bufs=2)
+                ress[s] = res
+            res = ress[s]
+            y = accs[(s, b)][:].rearrange("p (q e j) -> p q e j", q=2, e=2)
+            t1 = work.tile([P, 2, 2, NJ], F32, name="t1", tag="t1", bufs=4)
+            t2 = work.tile([P, 2, 2, NJ], F32, name="t2", tag="t2", bufs=4)
+            if s not in HEAVY:
+                nc.gpsimd.tensor_tensor(out=t2[:], in0=ysws[(s, b)][:],
+                                        in1=sz[:, s].unsqueeze(2).to_broadcast([P, 2, 2, NJ]),
+                                        op=ALU.mult)
+            nc.vector.tensor_tensor(out=t1[:], in0=y,
+                                    in1=cz[:, s].unsqueeze(2).to_broadcast([P, 2, 2, NJ]),
+                                    op=ALU.mult)
+            if s in HEAVY:
+                nc.vector.scalar_tensor_tensor(out=t2[:, :, 0, :], in0=y[:, :, 1, :], scalar=-1.0,
+                                               in1=sz[:, s], op0=ALU.mult, op1=ALU.mult)
+                nc.vector.tensor_tensor(out=t2[:, :, 1, :], in0=y[:, :, 0, :], in1=sz[:, s],
+                                        op=ALU.mult)
+            adder = nc.vector if (s == NT - 1 and b == B - 1) else nc.gpsimd
+            adder.tensor_tensor(out=res[:, b].rearrange("p q (j e) -> p q j e", e=2),
+                                in0=t1[:].rearrange("p q e j -> p q j e"),
+                                in1=t2[:].rearrange("p q e j -> p q j e"), op=ALU.add)
+            if s == NT - 1:
+                nc.sync.dma_start(out=oq[s][:, b], in_=res[:, b, 0, :])
+                nc.sync.dma_start(out=ok[s][:, b], in_=res[:, b, 1, :])
+            elif b == B - 1:
+                nc.sync.dma_start(out=oq[s], in_=res[:, :, 0, :])
+                nc.sync.dma_start(out=ok[s], in_=res[:, :, 1, :])
+
+        xbf0 = work.tile([P, B, H], BF16, name="xbf", tag="xbf", bufs=3)
+        xbfs[0] = xbf0
+        for g in range(NG):
+            nc.scalar.activation(out=xbf0[:, 0, 512 * g:512 * (g + 1)],
+                           in_=xb8[0][:, 0, 512 * g:512 * (g + 1)].bitcast(FP8), func=ACT.Copy)
+        for h in range(2):
+            nc.vector.tensor_copy(out=xbf0[:, 1, 1024 * h:1024 * (h + 1)],
+                                  in_=xb8[0][:, 1, 1024 * h:1024 * (h + 1)].bitcast(FP8))
+        arg = const.tile(TSH, F32, name="arg", tag="te")
+        nc.vector.tensor_tensor(out=arg[:], in0=lnc[:].unsqueeze(1).to_broadcast(TSH),
+                                in1=pc[:].unsqueeze(2).to_broadcast(TSH), op=ALU.mult)
+        for g in range(NG):
+            transposes(0, g)
+        for g in range(NG):
+            evacuate(0, g)
+            if g < 3:
+                reduce_angles(g)
+        cast(1, 4)
+        quantize(0, 0)
+        quantize(0, 1)
+        for g in range(NG):
+            transposes(1, g)
+        for g in range(NG):
+            evacuate(1, g)
+        quantize(1, 0)
+
+        for g in range(NG):
+            for m in range(2):
+                nc.gpsimd.tensor_scalar(
+                    out=wgqk[:, g, 1024 * m:1024 * (m + 1)].rearrange("p (e j t) -> p e j t", e=2, t=4),
+                    in0=wraw[m][:, g].rearrange("p t (j e) -> p e j t", e=2),
+                    scalar1=1.0, scalar2=0.0, op0=ALU.mult, op1=ALU.add)
+        for g in range(NG):
+            nc.vector.tensor_copy(out=wgv[:, g, :].rearrange("p (n t) -> p n t", t=4),
+                                  in_=wraw[2][:, g].rearrange("p t n -> p n t"))
+        cast(2, 1)
+        for g in range(NG):
+            transposes(2, g)
+
+        nc.scalar.activation(out=zz[:, :, 0, :], in_=arg[:], func=ACT.Exp)
+        nc.scalar.activation(out=zz[:, :, 1, :], in_=arg[:], func=ACT.Exp, scale=-1.0)
+        ab = const.tile(TSH, F32, name="ab", tag="ta")
+        nc.scalar.activation(out=ab[:], in_=red[:], func=ACT.Abs)
+        sn = const.tile(TSH, F32, name="sn", tag="tb")
+        nc.scalar.activation(out=sn[:], in_=red[:], func=ACT.Sin)
+        cs = const.tile(TSH, F32, name="cs", tag="te")
+        nc.scalar.activation(out=cs[:], in_=ab[:], func=ACT.Sin, scale=-1.0, bias=hpi[:, 0:1])
+        for h in range(NT // 2):
+            table_products(h)
+
+        for h in range(2):
+            nc.vector.quantize_mx(
+                out=wcqk[:, 2 * h:2 * h + 2, :].rearrange("p g c -> p (g c)").bitcast(FP8X4),
+                scales=wsqk[:, 2 * h:2 * h + 2, :].rearrange("p g c -> p (g c)"),
+                in_=wgqk[:, 2 * h:2 * h + 2, :].rearrange("p g c -> p (g c)"))
+        nc.vector.quantize_mx(out=wcv[:].rearrange("p g c -> p (g c)").bitcast(FP8X4),
+                              scales=wsv[:].rearrange("p g c -> p (g c)"),
+                              in_=wgv[:].rearrange("p g c -> p (g c)"))
+        cast(3, 1)
+        for k in range(4):
+            multiply(0, k)
+        swapped_copy(0, 0)
+        swapped_copy(0, 1)
+        v_out(0)
+
+        for i in range(NT):
+            if i + 4 < NT:
+                cast(i + 4, 1)
+            for k in range(4):
+                if i + 2 < NT:
+                    evacuate(i + 2, k)
+                if k == 1:
+                    if i + 1 < NT:
+                        quantize(i + 1, 1)
+                    rotate(i, 0)
+                if k == 3:
+                    if i + 2 < NT:
+                        quantize(i + 2, 0)
+                    rotate(i, 1)
+                if i + 3 < NT:
+                    transposes(i + 3, k)
+                if i + 1 < NT:
+                    multiply(i + 1, k)
+                    if k == 1:
+                        swapped_copy(i + 1, 0)
+                    if k == 3:
+                        swapped_copy(i + 1, 1)
+                        v_out(i + 1)

@@ -21,10 +21,9 @@ NG = H // 512
 NJ = DH // 2
 FLOPS = 2 * B * S * H * 3 * DH
 
-TWO_PI_HI = 6.28125
-TWO_PI_LO = 2.0 * math.pi - TWO_PI_HI
 FREQ_RATIO = 10000.0 ** (-1.0 / NJ)
 HEAVY = (0, 1, 2, 6, 7)
+JR = 4 * math.ceil(NJ * math.log((S - 1) / math.pi) / math.log(10000.0) / 4)
 
 
 def tile_retblock_pa_kernel(tc, x_bytes, x_scale, w_q, w_k, w_v, out_0, out_1, out_2):
@@ -94,24 +93,19 @@ def tile_retblock_pa_kernel(tc, x_bytes, x_scale, w_q, w_k, w_v, out_0, out_1, o
         ang = const.tile(TSH, F32, name="ang", tag="ta")
         nc.vector.tensor_tensor(out=ang[:], in0=th[:].unsqueeze(1).to_broadcast(TSH),
                                 in1=pos[:].unsqueeze(2).to_broadcast(TSH), op=ALU.mult)
-        ki = const.tile(TSH, I32, name="ki", tag="tb")
-        r1 = const.tile(TSH, F32, name="r1", tag="tc")
-        red = const.tile(TSH, F32, name="red", tag="td")
+        ki = const.tile([P, NT, JR], I32, name="ki", tag="tb")
 
         def reduce_angles(step):
             if step == 0:
-                nc.vector.tensor_scalar(out=ki[:], in0=ang[:], scalar1=1.0 / (2.0 * math.pi), scalar2=None,
+                nc.vector.tensor_scalar(out=ki[:], in0=ang[:, :, 0:JR], scalar1=1.0 / (2.0 * math.pi), scalar2=None,
                                         op0=ALU.mult)
             if step == 1:
-                nc.vector.scalar_tensor_tensor(out=r1[:], in0=ki[:], scalar=-TWO_PI_HI, in1=ang[:],
-                                               op0=ALU.mult, op1=ALU.add)
-            if step == 2:
-                nc.vector.scalar_tensor_tensor(out=red[:], in0=ki[:], scalar=-TWO_PI_LO, in1=r1[:],
-                                               op0=ALU.mult, op1=ALU.add)
+                nc.vector.scalar_tensor_tensor(out=ang[:, :, 0:JR], in0=ki[:], scalar=-2.0 * math.pi,
+                                               in1=ang[:, :, 0:JR], op0=ALU.mult, op1=ALU.add)
 
         zz = const.tile([P, NT, 2, NJ], F32, name="zz")
         cz = const.tile([P, NT, 2, NJ], F32, name="cz")
-        sz = const.tile([P, NT, 2, NJ], F32, name="sz")
+        sz = const.tile([P, NT, 2, 2, NJ], F32, name="sz")
 
         wgqk = const.tile([P, NG, 2048], BF16, name="wgqk", align_bytes=64)
         wgv = const.tile([P, NG, 1024], BF16, name="wgv", align_bytes=64)
@@ -193,8 +187,12 @@ def tile_retblock_pa_kernel(tc, x_bytes, x_scale, w_q, w_k, w_v, out_0, out_1, o
             ts = slice(2 * h, 2 * h + 2)
             nc.gpsimd.tensor_tensor(out=cz[:, ts], in0=cs[:, ts].unsqueeze(2).to_broadcast([P, 2, 2, NJ]),
                                     in1=zz[:, ts], op=ALU.mult)
-            nc.gpsimd.tensor_tensor(out=sz[:, ts], in0=sn[:, ts].unsqueeze(2).to_broadcast([P, 2, 2, NJ]),
+            nc.gpsimd.tensor_tensor(out=sz[:, ts, 1], in0=sn[:, ts].unsqueeze(2).to_broadcast([P, 2, 2, NJ]),
                                     in1=zz[:, ts], op=ALU.mult)
+
+        def negate(h):
+            ts = slice(2 * h, 2 * h + 2)
+            nc.scalar.activation(out=sz[:, ts, 0], in_=sz[:, ts, 1], func=ACT.Copy, scale=-1.0)
 
         oq = out_0.rearrange("b (s p) c -> s p b c", p=P)
         ok = out_1.rearrange("b (s p) c -> s p b c", p=P)
@@ -204,10 +202,9 @@ def tile_retblock_pa_kernel(tc, x_bytes, x_scale, w_q, w_k, w_v, out_0, out_1, o
             if s in HEAVY:
                 return
             y = accs[(s, b)][:].rearrange("p (q e j) -> p q e j", q=2, e=2)
-            ysw = work.tile([P, 2, 2, NJ], F32, name="ysw", tag="ysw", bufs=4)
+            ysw = work.tile([P, 2, NJ, 2], F32, name="ysw", tag="ysw", bufs=3)
             ysws[(s, b)] = ysw
-            nc.scalar.activation(out=ysw[:, :, 0, :], in_=y[:, :, 1, :], func=ACT.Copy, scale=-1.0)
-            nc.scalar.copy(out=ysw[:, :, 1, :], in_=y[:, :, 0, :])
+            nc.scalar.copy(out=ysw[:], in_=y[:, :, ::-1, :].rearrange("p q e j -> p q j e"))
 
         def v_out(s):
             resv = work.tile([P, B, DH], F32, name="resv", tag="resv", bufs=2)
@@ -220,24 +217,18 @@ def tile_retblock_pa_kernel(tc, x_bytes, x_scale, w_q, w_k, w_v, out_0, out_1, o
                 ress[s] = res
             res = ress[s]
             y = accs[(s, b)][:].rearrange("p (q e j) -> p q e j", q=2, e=2)
-            t1 = work.tile([P, 2, 2, NJ], F32, name="t1", tag="t1", bufs=4)
-            t2 = work.tile([P, 2, 2, NJ], F32, name="t2", tag="t2", bufs=4)
+            t1 = work.tile([P, 2, NJ, 2], F32, name="t1", tag="t1", bufs=3)
+            t2 = work.tile([P, 2, NJ, 2], F32, name="t2", tag="t2", bufs=3)
+            szs = sz[:, s].rearrange("p e q j -> p q j e")
             if s not in HEAVY:
-                nc.gpsimd.tensor_tensor(out=t2[:], in0=ysws[(s, b)][:],
-                                        in1=sz[:, s].unsqueeze(2).to_broadcast([P, 2, 2, NJ]),
-                                        op=ALU.mult)
-            nc.vector.tensor_tensor(out=t1[:], in0=y,
-                                    in1=cz[:, s].unsqueeze(2).to_broadcast([P, 2, 2, NJ]),
-                                    op=ALU.mult)
+                nc.gpsimd.tensor_tensor(out=t2[:], in0=ysws[(s, b)][:], in1=szs, op=ALU.mult)
+            nc.vector.tensor_tensor(out=t1[:], in0=y.rearrange("p q e j -> p q j e"),
+                                    in1=cz[:, s].unsqueeze(3).to_broadcast([P, 2, NJ, 2]), op=ALU.mult)
             if s in HEAVY:
-                nc.vector.scalar_tensor_tensor(out=t2[:, :, 0, :], in0=y[:, :, 1, :], scalar=-1.0,
-                                               in1=sz[:, s], op0=ALU.mult, op1=ALU.mult)
-                nc.vector.tensor_tensor(out=t2[:, :, 1, :], in0=y[:, :, 0, :], in1=sz[:, s],
+                nc.vector.tensor_tensor(out=t2[:], in0=y[:, :, ::-1, :].rearrange("p q e j -> p q j e"), in1=szs,
                                         op=ALU.mult)
             adder = nc.vector if (s == NT - 1 and b == B - 1) else nc.gpsimd
-            adder.tensor_tensor(out=res[:, b].rearrange("p q (j e) -> p q j e", e=2),
-                                in0=t1[:].rearrange("p q e j -> p q j e"),
-                                in1=t2[:].rearrange("p q e j -> p q j e"), op=ALU.add)
+            adder.tensor_tensor(out=res[:, b].rearrange("p q (j e) -> p q j e", e=2), in0=t1[:], in1=t2[:], op=ALU.add)
             if s == NT - 1:
                 nc.sync.dma_start(out=oq[s][:, b], in_=res[:, b, 0, :])
                 nc.sync.dma_start(out=ok[s][:, b], in_=res[:, b, 1, :])
@@ -260,7 +251,7 @@ def tile_retblock_pa_kernel(tc, x_bytes, x_scale, w_q, w_k, w_v, out_0, out_1, o
             transposes(0, g)
         for g in range(NG):
             evacuate(0, g)
-            if g < 3:
+            if g < 2:
                 reduce_angles(g)
         cast(1, 4)
         quantize(0, 0)
@@ -277,19 +268,18 @@ def tile_retblock_pa_kernel(tc, x_bytes, x_scale, w_q, w_k, w_v, out_0, out_1, o
                     out=wgqk[:, g, 1024 * m:1024 * (m + 1)].rearrange("p (e j t) -> p e j t", e=2, t=4),
                     in0=wraw[m][:, g].rearrange("p t (j e) -> p e j t", e=2),
                     scalar1=1.0, scalar2=0.0, op0=ALU.mult, op1=ALU.add)
-        for g in range(NG):
-            nc.vector.tensor_copy(out=wgv[:, g, :].rearrange("p (n t) -> p n t", t=4),
-                                  in_=wraw[2][:, g].rearrange("p t n -> p n t"))
+        nc.vector.tensor_copy(out=wgv[:].rearrange("p g (n t) -> p g n t", t=4),
+                              in_=wraw[2][:].rearrange("p g t n -> p g n t"))
         cast(2, 1)
         for g in range(NG):
             transposes(2, g)
 
         nc.scalar.activation(out=zz[:, :, 0, :], in_=arg[:], func=ACT.Exp)
         nc.scalar.activation(out=zz[:, :, 1, :], in_=arg[:], func=ACT.Exp, scale=-1.0)
-        ab = const.tile(TSH, F32, name="ab", tag="ta")
-        nc.scalar.activation(out=ab[:], in_=red[:], func=ACT.Abs)
-        sn = const.tile(TSH, F32, name="sn", tag="tb")
-        nc.scalar.activation(out=sn[:], in_=red[:], func=ACT.Sin)
+        ab = const.tile(TSH, F32, name="ab", tag="tc")
+        nc.scalar.activation(out=ab[:], in_=ang[:], func=ACT.Abs)
+        sn = const.tile(TSH, F32, name="sn", tag="td")
+        nc.scalar.activation(out=sn[:], in_=ang[:], func=ACT.Sin)
         cs = const.tile(TSH, F32, name="cs", tag="te")
         nc.scalar.activation(out=cs[:], in_=ab[:], func=ACT.Sin, scale=-1.0, bias=hpi[:, 0:1])
         for h in range(NT // 2):
@@ -304,6 +294,7 @@ def tile_retblock_pa_kernel(tc, x_bytes, x_scale, w_q, w_k, w_v, out_0, out_1, o
                               scales=wsv[:].rearrange("p g c -> p (g c)"),
                               in_=wgv[:].rearrange("p g c -> p (g c)"))
         cast(3, 1)
+        negate(0)
         for k in range(4):
             multiply(0, k)
         swapped_copy(0, 0)
@@ -313,6 +304,8 @@ def tile_retblock_pa_kernel(tc, x_bytes, x_scale, w_q, w_k, w_v, out_0, out_1, o
         for i in range(NT):
             if i + 4 < NT:
                 cast(i + 4, 1)
+            if i < 3:
+                negate(i + 1)
             for k in range(4):
                 if i + 2 < NT:
                     evacuate(i + 2, k)

@@ -22,7 +22,10 @@ NJ = DH // 2
 FLOPS = 2 * B * S * H * 3 * DH
 
 FREQ_RATIO = 10000.0 ** (-1.0 / NJ)
-HEAVY = (0, 1, 2, 6, 7)
+HEAVY = (0, 1, 2, 3, 4, 5, 6, 7)
+OFF = 3
+PK = 0
+OFFS = (5, 6, 7)
 JR = 4 * math.ceil(NJ * math.log((S - 1) / math.pi) / math.log(10000.0) / 4)
 
 
@@ -115,6 +118,7 @@ def tile_retblock_pa_kernel(tc, x_bytes, x_scale, w_q, w_k, w_v, out_0, out_1, o
         wsv = const.tile([P, NG, 256], U8, name="wsv", align_bytes=64)
 
         xbfs, xts, grps, xcs, xss, accs, accvs, ysws, ress = {}, {}, {}, {}, {}, {}, {}, {}, {}
+        pls = {}
 
         def cast(s, chunks):
             xbf = work.tile([P, B, H], BF16, name="xbf", tag="xbf", bufs=3)
@@ -151,6 +155,19 @@ def tile_retblock_pa_kernel(tc, x_bytes, x_scale, w_q, w_k, w_v, out_0, out_1, o
                 op=ALU.mult,
             )
 
+        def planes_out(s, g):
+            pl = work.tile([P, 4, B * P], BF16, name="pl", tag="pl", bufs=2)
+            pls[s] = pl
+            bank = xts[(s, g)][:].rearrange("p u r -> p (u r)").bitcast(BF16).rearrange("p (u r e) -> p u e r", u=2, e=2)
+            for t in range(4):
+                nc.scalar.activation(out=pl[:, t], in_=bank[:, t // 2, t % 2], func=ACT.Copy,
+                                     scale=scl[:, 4 * g + t:4 * g + t + 1])
+
+        def interleave_x(s, g):
+            nc.gpsimd.tensor_scalar(out=grps[s][:, g, :].rearrange("p (r t) -> p r t", t=4),
+                                    in0=pls[s][:].rearrange("p t r -> p r t"),
+                                    scalar1=1.0, scalar2=0.0, op0=ALU.mult, op1=ALU.add)
+
         def quantize(s, h):
             if h == 0:
                 xc = work.tile([P, NG, B * P], U32, name="xc", tag="xc", bufs=4, align_bytes=64)
@@ -185,9 +202,9 @@ def tile_retblock_pa_kernel(tc, x_bytes, x_scale, w_q, w_k, w_v, out_0, out_1, o
 
         def table_products(h):
             ts = slice(2 * h, 2 * h + 2)
-            nc.gpsimd.tensor_tensor(out=cz[:, ts], in0=cs[:, ts].unsqueeze(2).to_broadcast([P, 2, 2, NJ]),
-                                    in1=zz[:, ts], op=ALU.mult)
             nc.gpsimd.tensor_tensor(out=sz[:, ts, 1], in0=sn[:, ts].unsqueeze(2).to_broadcast([P, 2, 2, NJ]),
+                                    in1=zz[:, ts], op=ALU.mult)
+            nc.gpsimd.tensor_tensor(out=cz[:, ts], in0=cs[:, ts].unsqueeze(2).to_broadcast([P, 2, 2, NJ]),
                                     in1=zz[:, ts], op=ALU.mult)
 
         def negate(h):
@@ -268,18 +285,21 @@ def tile_retblock_pa_kernel(tc, x_bytes, x_scale, w_q, w_k, w_v, out_0, out_1, o
                     out=wgqk[:, g, 1024 * m:1024 * (m + 1)].rearrange("p (e j t) -> p e j t", e=2, t=4),
                     in0=wraw[m][:, g].rearrange("p t (j e) -> p e j t", e=2),
                     scalar1=1.0, scalar2=0.0, op0=ALU.mult, op1=ALU.add)
-        nc.vector.tensor_copy(out=wgv[:].rearrange("p g (n t) -> p g n t", t=4),
-                              in_=wraw[2][:].rearrange("p g t n -> p g n t"))
+        for g in range(2):
+            nc.scalar.copy(out=wgv[:, g].rearrange("p (n t) -> p n t", t=4),
+                           in_=wraw[2][:, g].rearrange("p t n -> p n t"))
+        nc.vector.tensor_copy(out=wgv[:, 2:4].rearrange("p g (n t) -> p g n t", t=4),
+                              in_=wraw[2][:, 2:4].rearrange("p g t n -> p g n t"))
         cast(2, 1)
         for g in range(NG):
             transposes(2, g)
 
         nc.scalar.activation(out=zz[:, :, 0, :], in_=arg[:], func=ACT.Exp)
         nc.scalar.activation(out=zz[:, :, 1, :], in_=arg[:], func=ACT.Exp, scale=-1.0)
-        ab = const.tile(TSH, F32, name="ab", tag="tc")
-        nc.scalar.activation(out=ab[:], in_=ang[:], func=ACT.Abs)
         sn = const.tile(TSH, F32, name="sn", tag="td")
         nc.scalar.activation(out=sn[:], in_=ang[:], func=ACT.Sin)
+        ab = const.tile(TSH, F32, name="ab", tag="tc")
+        nc.scalar.activation(out=ab[:], in_=ang[:], func=ACT.Abs)
         cs = const.tile(TSH, F32, name="cs", tag="te")
         nc.scalar.activation(out=cs[:], in_=ab[:], func=ACT.Sin, scale=-1.0, bias=hpi[:, 0:1])
         for h in range(NT // 2):
@@ -293,8 +313,8 @@ def tile_retblock_pa_kernel(tc, x_bytes, x_scale, w_q, w_k, w_v, out_0, out_1, o
         nc.vector.quantize_mx(out=wcv[:].rearrange("p g c -> p (g c)").bitcast(FP8X4),
                               scales=wsv[:].rearrange("p g c -> p (g c)"),
                               in_=wgv[:].rearrange("p g c -> p (g c)"))
-        cast(3, 1)
         negate(0)
+        cast(3, 1)
         for k in range(4):
             multiply(0, k)
         swapped_copy(0, 0)
@@ -308,7 +328,12 @@ def tile_retblock_pa_kernel(tc, x_bytes, x_scale, w_q, w_k, w_v, out_0, out_1, o
                 negate(i + 1)
             for k in range(4):
                 if i + 2 < NT:
-                    evacuate(i + 2, k)
+                    if k == OFF and i + 2 in OFFS:
+                        interleave_x(i + 2, k)
+                    else:
+                        evacuate(i + 2, k)
+                if k == PK and i + 2 in OFFS:
+                    planes_out(i + 2, OFF)
                 if k == 1:
                     if i + 1 < NT:
                         quantize(i + 1, 1)

from contextlib import ExitStack
import math

import concourse.mybir as mybir
from concourse.masks import make_identity

F32 = mybir.dt.float32
BF16 = mybir.dt.bfloat16
U8 = mybir.dt.uint8
U32 = mybir.dt.uint32
I32 = mybir.dt.int32
FP8 = mybir.dt.float8_e4m3fn
FP8X4 = mybir.dt.float8_e4m3fn_x4
ALU = mybir.AluOpType
ACT = mybir.ActivationFunctionType

B, S, H, DH = 2, 1024, 2048, 256
P = 128
NT = S // P
NG = H // 512
NJ = DH // 2
FLOPS = 2 * B * S * H * 3 * DH

FREQ_RATIO = 10000.0 ** (-1.0 / NJ)
HEAVY = (0, 1, 2, 3, 4, 5, 6, 7)
OFF = 3
PK = 0
OFFS = (5, 6, 7)
JR = 4 * math.ceil(NJ * math.log((S - 1) / math.pi) / math.log(10000.0) / 4)


def tile_retblock_pa_kernel(tc, x_bytes, x_scale, w_q, w_k, w_v, out_0, out_1, out_2):
    nc = tc.nc
    with ExitStack() as ctx:
        const = ctx.enter_context(tc.tile_pool(name="const", bufs=1))
        work = ctx.enter_context(tc.tile_pool(name="work", bufs=2))
        psx = ctx.enter_context(tc.psum_pool(name="psx", bufs=4))
        psa = ctx.enter_context(tc.psum_pool(name="psa", bufs=3))
        psv = ctx.enter_context(tc.psum_pool(name="psv", bufs=1))
        ctx.enter_context(tc.manual_schedule())

        xv = x_bytes.rearrange("b (s p) k -> s p b k", p=P)
        xb8 = []
        for s in range(NT):
            xbytes = const.tile([P, B, H], U8, name="xbytes%d" % s)
            xb8.append(xbytes)
        wraw = []
        for m in range(3):
            wr = const.tile([P, NG, 4, DH], BF16, name="wraw%d" % m)
            wraw.append(wr)
        for g in range(NG):
            nc.sync.dma_start(out=xb8[0][:, :, 512 * g:512 * (g + 1)], in_=xv[0][:, :, 512 * g:512 * (g + 1)])
        scl = const.tile([P, NG * 4], F32, name="scl")
        nc.sync.dma_start(
            out=scl[:].rearrange("p (g t) -> p g t", t=4),
            in_=x_scale.rearrange("a b k -> (a b k)").rearrange("(g p t) -> p g t", p=P, t=4),
        )
        nc.sync.dma_start(out=xb8[1][:], in_=xv[1])
        for g in range(NG):
            for m, w in enumerate((w_q, w_k, w_v)):
                nc.sync.dma_start(
                    out=wraw[m][:, g], in_=w.rearrange("(g p t) n -> p g t n", p=P, t=4)[:, g]
                )
        for s in range(2, NT):
            nc.sync.dma_start(out=xb8[s][:], in_=xv[s])

        ident = const.tile([P, P], F32, name="ident")
        make_identity(nc, ident[:])
        pos = const.tile([P, NT], F32, name="pos")
        nc.gpsimd.iota(pos[:], pattern=[[P, NT]], base=0, channel_multiplier=1,
                       allow_small_or_imprecise_dtypes=True)
        jj = const.tile([P, NJ], F32, name="jj")
        nc.gpsimd.iota(jj[:], pattern=[[1, NJ]], base=0, channel_multiplier=0,
                       allow_small_or_imprecise_dtypes=True)

        th = const.tile([P, NJ], F32, name="th")
        nc.vector.memset(th[:, 0:1], 1.0)
        m = 1
        while m < NJ:
            nc.vector.tensor_scalar(out=th[:, m:2 * m], in0=th[:, 0:m], scalar1=FREQ_RATIO ** m,
                                    scalar2=None, op0=ALU.mult)
            m *= 2
        cj = const.tile([P, NJ], F32, name="cj")
        nc.vector.tensor_scalar(out=cj[:], in0=jj[:], scalar1=2.0 / (1.4 * DH),
                                scalar2=(0.4 * DH) / (1.4 * DH), op0=ALU.mult, op1=ALU.add)
        pc = const.tile([P, NT], F32, name="pc")
        nc.vector.tensor_scalar(out=pc[:], in0=pos[:], scalar1=-0.5 * S, scalar2=1.0 / 512.0,
                                op0=ALU.add, op1=ALU.mult)
        hpi = const.tile([P, 1], F32, name="hpi")
        nc.vector.tensor_scalar(out=hpi[:], in0=th[:, 0:1], scalar1=0.5 * math.pi, scalar2=None,
                                op0=ALU.mult)
        lnc = const.tile([P, NJ], F32, name="lnc")
        nc.scalar.activation(out=lnc[:], in_=cj[:], func=ACT.Ln)

        TSH = [P, NT, NJ]
        ang = const.tile(TSH, F32, name="ang", tag="ta")
        nc.vector.tensor_tensor(out=ang[:], in0=th[:].unsqueeze(1).to_broadcast(TSH),
                                in1=pos[:].unsqueeze(2).to_broadcast(TSH), op=ALU.mult)
        ki = const.tile([P, NT, JR], I32, name="ki", tag="tb")

        def reduce_angles(step):
            if step == 0:
                nc.vector.tensor_scalar(out=ki[:], in0=ang[:, :, 0:JR], scalar1=1.0 / (2.0 * math.pi), scalar2=None,
                                        op0=ALU.mult)
            if step == 1:
                nc.vector.scalar_tensor_tensor(out=ang[:, :, 0:JR], in0=ki[:], scalar=-2.0 * math.pi,
                                               in1=ang[:, :, 0:JR], op0=ALU.mult, op1=ALU.add)

        zz = const.tile([P, NT, 2, NJ], F32, name="zz")
        cz = const.tile([P, NT, 2, NJ], F32, name="cz")
        sz = const.tile([P, NT, 2, 2, NJ], F32, name="sz")

        wgqk = const.tile([P, NG, 2048], BF16, name="wgqk", align_bytes=64)
        wgv = const.tile([P, NG, 1024], BF16, name="wgv", align_bytes=64)
        wcqk = const.tile([P, NG, 512], U32, name="wcqk", align_bytes=64)
        wsqk = const.tile([P, NG, 512], U8, name="wsqk", align_bytes=64)
        wcv = const.tile([P, NG, 256], U32, name="wcv", align_bytes=64)
        wsv = const.tile([P, NG, 256], U8, name="wsv", align_bytes=64)

        xbfs, xts, grps, xcs, xss, accs, accvs, ysws, ress = {}, {}, {}, {}, {}, {}, {}, {}, {}
        pls = {}

        def cast(s, chunks):
            xbf = work.tile([P, B, H], BF16, name="xbf", tag="xbf", bufs=3)
            xbfs[s] = xbf
            w = H // chunks
            if chunks == 1:
                nc.scalar.activation(out=xbf[:].rearrange("p b k -> p (b k)"),
                               in_=xb8[s][:].rearrange("p b k -> p (b k)").bitcast(FP8), func=ACT.Copy)
            else:
                for c in range(chunks):
                    for b in range(B):
                        nc.scalar.activation(out=xbf[:, b, c * w:(c + 1) * w],
                                       in_=xb8[s][:, b, c * w:(c + 1) * w].bitcast(FP8), func=ACT.Copy)

        def transposes(s, g):
            xt = psx.tile([P, 2, B * P], F32, name="xt", tag="xt")
            xts[(s, g)] = xt
            for b in range(B):
                words = xbfs[s][:, b, :].bitcast(F32)
                for u in range(2):
                    nc.tensor.transpose(xt[:, u, P * b:P * (b + 1)],
                                        words[:, 256 * g + u:256 * (g + 1):2], ident[:])

        def evacuate(s, g):
            if g == 0:
                grp = work.tile([P, NG, 1024], BF16, name="grp", tag="grp", bufs=2, align_bytes=64)
                grps[s] = grp
            nc.vector.tensor_tensor(
                out=grps[s][:, g, :].rearrange("p (r u e) -> p r u e", u=2, e=2),
                in0=xts[(s, g)][:].rearrange("p u r -> p (u r)").bitcast(BF16).rearrange(
                    "p (u r e) -> p r u e", u=2, e=2),
                in1=scl[:, 4 * g:4 * g + 4].rearrange("p (u e) -> p u e", u=2).unsqueeze(1)
                .to_broadcast([P, B * P, 2, 2]),
                op=ALU.mult,
            )

        def planes_out(s, g):
            pl = work.tile([P, 4, B * P], BF16, name="pl", tag="pl", bufs=2)
            pls[s] = pl
            bank = xts[(s, g)][:].rearrange("p u r -> p (u r)").bitcast(BF16).rearrange("p (u r e) -> p u e r", u=2, e=2)
            for t in range(4):
                nc.scalar.activation(out=pl[:, t], in_=bank[:, t // 2, t % 2], func=ACT.Copy,
                                     scale=scl[:, 4 * g + t:4 * g + t + 1])

        def interleave_x(s, g):
            nc.gpsimd.tensor_scalar(out=grps[s][:, g, :].rearrange("p (r t) -> p r t", t=4),
                                    in0=pls[s][:].rearrange("p t r -> p r t"),
                                    scalar1=1.0, scalar2=0.0, op0=ALU.mult, op1=ALU.add)

        def quantize(s, h):
            if h == 0:
                xc = work.tile([P, NG, B * P], U32, name="xc", tag="xc", bufs=4, align_bytes=64)
                xs = work.tile([P, NG, B * P], U8, name="xs", tag="xs", bufs=4, align_bytes=64)
                xcs[s], xss[s] = xc, xs
            gs = slice(2 * h, 2 * h + 2)
            nc.vector.quantize_mx(
                out=xcs[s][:, gs, :].rearrange("p g c -> p (g c)").bitcast(FP8X4),
                scales=xss[s][:, gs, :].rearrange("p g c -> p (g c)"),
                in_=grps[s][:, gs, :].rearrange("p g c -> p (g c)"),
            )

        def multiply(s, k):
            xc, xs = xcs[s], xss[s]
            b, h = k // 2, k % 2
            if k == 0:
                accv = psv.tile([P, B, DH], F32, name="accv", tag="accv")
                accvs[s] = accv
            if h == 0:
                acc = psa.tile([P, 2 * DH], F32, name="acc", tag="acc")
                accs[(s, b)] = acc
            cols = slice(P * b, P * (b + 1))
            for g in (2 * h, 2 * h + 1):
                nc.tensor.matmul_mx(out=accs[(s, b)][:], lhsT=xc[:, g, cols].bitcast(FP8X4),
                                    lhsT_scale=xs[:, g, cols],
                                    rhs=wcqk[:, g, :].bitcast(FP8X4), rhs_scale=wsqk[:, g, :],
                                    start=(g == 0), stop=(g == NG - 1))
                nc.tensor.matmul_mx(out=accvs[s][:, b, :], lhsT=xc[:, g, cols].bitcast(FP8X4),
                                    lhsT_scale=xs[:, g, cols],
                                    rhs=wcv[:, g, :].bitcast(FP8X4), rhs_scale=wsv[:, g, :],
                                    start=(g == 0), stop=(g == NG - 1))

        def table_products(h):
            ts = slice(2 * h, 2 * h + 2)
            nc.gpsimd.tensor_tensor(out=sz[:, ts, 1], in0=sn[:, ts].unsqueeze(2).to_broadcast([P, 2, 2, NJ]),
                                    in1=zz[:, ts], op=ALU.mult)
            nc.gpsimd.tensor_tensor(out=cz[:, ts], in0=cs[:, ts].unsqueeze(2).to_broadcast([P, 2, 2, NJ]),
                                    in1=zz[:, ts], op=ALU.mult)

        def negate(h):
            ts = slice(2 * h, 2 * h + 2)
            nc.scalar.activation(out=sz[:, ts, 0], in_=sz[:, ts, 1], func=ACT.Copy, scale=-1.0)

        oq = out_0.rearrange("b (s p) c -> s p b c", p=P)
        ok = out_1.rearrange("b (s p) c -> s p b c", p=P)
        ov = out_2.rearrange("b (s p) c -> s p b c", p=P)

        def swapped_copy(s, b):
            if s in HEAVY:
                return
            y = accs[(s, b)][:].rearrange("p (q e j) -> p q e j", q=2, e=2)
            ysw = work.tile([P, 2, NJ, 2], F32, name="ysw", tag="ysw", bufs=3)
            ysws[(s, b)] = ysw
            nc.scalar.copy(out=ysw[:], in_=y[:, :, ::-1, :].rearrange("p q e j -> p q j e"))

        def v_out(s):
            resv = work.tile([P, B, DH], F32, name="resv", tag="resv", bufs=2)
            nc.scalar.copy(out=resv[:], in_=accvs[s][:])
            nc.sync.dma_start(out=ov[s], in_=resv[:])

        def rotate(s, b):
            if b == 0:
                res = work.tile([P, B, 2, DH], F32, name="res", tag="res", bufs=2)
                ress[s] = res
            res = ress[s]
            y = accs[(s, b)][:].rearrange("p (q e j) -> p q e j", q=2, e=2)
            t1 = work.tile([P, 2, NJ, 2], F32, name="t1", tag="t1", bufs=3)
            t2 = work.tile([P, 2, NJ, 2], F32, name="t2", tag="t2", bufs=3)
            szs = sz[:, s].rearrange("p e q j -> p q j e")
            if s not in HEAVY:
                nc.gpsimd.tensor_tensor(out=t2[:], in0=ysws[(s, b)][:], in1=szs, op=ALU.mult)
            nc.vector.tensor_tensor(out=t1[:], in0=y.rearrange("p q e j -> p q j e"),
                                    in1=cz[:, s].unsqueeze(3).to_broadcast([P, 2, NJ, 2]), op=ALU.mult)
            if s in HEAVY:
                nc.vector.tensor_tensor(out=t2[:], in0=y[:, :, ::-1, :].rearrange("p q e j -> p q j e"), in1=szs,
                                        op=ALU.mult)
            adder = nc.vector if (s == NT - 1 and b == B - 1) else nc.gpsimd
            adder.tensor_tensor(out=res[:, b].rearrange("p q (j e) -> p q j e", e=2), in0=t1[:], in1=t2[:], op=ALU.add)
            if s == NT - 1:
                nc.sync.dma_start(out=oq[s][:, b], in_=res[:, b, 0, :])
                nc.sync.dma_start(out=ok[s][:, b], in_=res[:, b, 1, :])
            elif b == B - 1:
                nc.sync.dma_start(out=oq[s], in_=res[:, :, 0, :])
                nc.sync.dma_start(out=ok[s], in_=res[:, :, 1, :])

        xbf0 = work.tile([P, B, H], BF16, name="xbf", tag="xbf", bufs=3)
        xbfs[0] = xbf0
        for g in range(NG):
            nc.scalar.activation(out=xbf0[:, 0, 512 * g:512 * (g + 1)],
                           in_=xb8[0][:, 0, 512 * g:512 * (g + 1)].bitcast(FP8), func=ACT.Copy)
        for h in range(2):
            nc.vector.tensor_copy(out=xbf0[:, 1, 1024 * h:1024 * (h + 1)],
                                  in_=xb8[0][:, 1, 1024 * h:1024 * (h + 1)].bitcast(FP8))
        arg = const.tile(TSH, F32, name="arg", tag="te")
        nc.vector.tensor_tensor(out=arg[:], in0=lnc[:].unsqueeze(1).to_broadcast(TSH),
                                in1=pc[:].unsqueeze(2).to_broadcast(TSH), op=ALU.mult)
        for g in range(NG):
            transposes(0, g)
        for g in range(NG):
            evacuate(0, g)
            if g < 2:
                reduce_angles(g)
        cast(1, 4)
        quantize(0, 0)
        quantize(0, 1)
        for g in range(NG):
            transposes(1, g)
        for g in range(NG):
            evacuate(1, g)
        quantize(1, 0)

        for g in range(NG):
            for m in range(2):
                nc.gpsimd.tensor_scalar(
                    out=wgqk[:, g, 1024 * m:1024 * (m + 1)].rearrange("p (e j t) -> p e j t", e=2, t=4),
                    in0=wraw[m][:, g].rearrange("p t (j e) -> p e j t", e=2),
                    scalar1=1.0, scalar2=0.0, op0=ALU.mult, op1=ALU.add)
        for g in range(2):
            nc.scalar.copy(out=wgv[:, g].rearrange("p (n t) -> p n t", t=4),
                           in_=wraw[2][:, g].rearrange("p t n -> p n t"))
        nc.vector.tensor_copy(out=wgv[:, 2:4].rearrange("p g (n t) -> p g n t", t=4),
                              in_=wraw[2][:, 2:4].rearrange("p g t n -> p g n t"))
        cast(2, 1)
        for g in range(NG):
            transposes(2, g)

        nc.scalar.activation(out=zz[:, :, 0, :], in_=arg[:], func=ACT.Exp)
        nc.scalar.activation(out=zz[:, :, 1, :], in_=arg[:], func=ACT.Exp, scale=-1.0)
        sn = const.tile(TSH, F32, name="sn", tag="td")
        nc.scalar.activation(out=sn[:], in_=ang[:], func=ACT.Sin)
        ab = const.tile(TSH, F32, name="ab", tag="tc")
        nc.scalar.activation(out=ab[:], in_=ang[:], func=ACT.Abs)
        cs = const.tile(TSH, F32, name="cs", tag="te")
        nc.scalar.activation(out=cs[:], in_=ab[:], func=ACT.Sin, scale=-1.0, bias=hpi[:, 0:1])
        for h in range(NT // 2):
            table_products(h)

        for h in range(2):
            nc.vector.quantize_mx(
                out=wcqk[:, 2 * h:2 * h + 2, :].rearrange("p g c -> p (g c)").bitcast(FP8X4),
                scales=wsqk[:, 2 * h:2 * h + 2, :].rearrange("p g c -> p (g c)"),
                in_=wgqk[:, 2 * h:2 * h + 2, :].rearrange("p g c -> p (g c)"))
        nc.vector.quantize_mx(out=wcv[:].rearrange("p g c -> p (g c)").bitcast(FP8X4),
                              scales=wsv[:].rearrange("p g c -> p (g c)"),
                              in_=wgv[:].rearrange("p g c -> p (g c)"))
        negate(0)
        cast(3, 1)
        for k in range(4):
            multiply(0, k)
        swapped_copy(0, 0)
        swapped_copy(0, 1)
        v_out(0)

        for i in range(NT):
            if i + 4 < NT:
                cast(i + 4, 1)
            if i < 3:
                negate(i + 1)
            for k in range(4):
                if i + 2 < NT:
                    if k == OFF and i + 2 in OFFS:
                        interleave_x(i + 2, k)
                    else:
                        evacuate(i + 2, k)
                if k == PK and i + 2 in OFFS:
                    planes_out(i + 2, OFF)
                if k == 1:
                    if i + 1 < NT:
                        quantize(i + 1, 1)
                    rotate(i, 0)
                if k == 3:
                    if i + 2 < NT:
                        quantize(i + 2, 0)
                    rotate(i, 1)
                if i + 3 < NT:
                    transposes(i + 3, k)
                if i + 1 < NT:
                    multiply(i + 1, k)
                    if k == 1:
                        swapped_copy(i + 1, 0)
                    if k == 3:
                        swapped_copy(i + 1, 1)
                        v_out(i + 1)
